import numpy as np
import ml_dtypes


def mxq(x, axis, fmt="e4m3"):
    dtype, down = {"e4m3": (ml_dtypes.float8_e4m3fn, 7), "e5m2": (ml_dtypes.float8_e5m2, 14)}[fmt]
    v = np.moveaxis(np.asarray(x, np.float32).astype(ml_dtypes.bfloat16).astype(np.float64), axis, -1)
    blocks = v.reshape(v.shape[:-1] + (-1, 32))
    amax = np.abs(blocks).max(-1, keepdims=True)
    byte = np.maximum(np.where(amax > 0, np.frexp(amax)[1] - 1 + 127, 0) - down, 1)
    scale = np.exp2(byte - 127.0)
    codes = (blocks / scale).astype(np.float32).astype(dtype).astype(np.float64)
    return np.moveaxis((codes * scale).reshape(v.shape), -1, axis)


WIDE = False


def mx_kscale(k):
    if not WIDE:
        return np.ones(k)
    levels = np.array([20, -20, 10, -10, 0])
    a = np.random.permutation(np.resize(levels, k // 512 * 4)).reshape(k // 512, 4)
    idx = np.arange(k)
    return np.exp2(a[idx // 512, idx % 128 // 32])


BF16 = ml_dtypes.bfloat16


def bf(x):
    return np.asarray(x, np.float32).astype(BF16)


def f64(x):
    return np.asarray(x).astype(np.float64)


B, IN, H = 1024, 1024, 1024


def sigmoid(v):
    return 1.0 / (1.0 + np.exp(-v))


def setup_inputs():
    s = mx_kscale(B)[:, None]
    input0 = bf(np.random.standard_normal((B, IN)))
    state = bf(np.random.standard_normal((B, H)))
    c = bf(np.tanh(np.random.standard_normal((B, H))))
    W2 = bf(np.random.standard_normal((IN, H)) * 0.7 / np.sqrt(IN))
    U2 = bf(np.random.standard_normal((H, H)) * 0.7 / np.sqrt(H))
    bias_gate = bf(np.random.standard_normal((1, H)) * 0.5)
    g = bf(np.random.standard_normal((B, H)) * np.exp2(np.random.randint(-12, 1, (B, 1))) / s)
    z = sigmoid(f64(input0) @ f64(W2) + f64(state) @ f64(U2) + f64(bias_gate))
    return {'input': bf(f64(input0) * s),
            'state': state,
            'c': c,
            'W2': W2,
            'U2': U2,
            'bias_gate': bias_gate,
            'z': np.asarray(z, np.float32),
            'grad_out': g}


def reference(input, state, c, W2, U2, bias_gate, z, grad_out):
    zf = f64(z)
    da = f64(grad_out) * (f64(state) - f64(c)) * zf * (1.0 - zf)
    return mxq(f64(input), 0, 'e4m3').T @ mxq(da, 0, 'e5m2')

@@ -1,0 +1,207 @@
+from contextlib import ExitStack
+
+import concourse.mybir as mybir
+
+F32 = mybir.dt.float32
+BF16 = mybir.dt.bfloat16
+U32 = mybir.dt.uint32
+U8 = mybir.dt.uint8
+E4M3_X4 = mybir.dt.float8_e4m3fn_x4
+E5M2_X4 = mybir.dt.float8_e5m2_x4
+ALU = mybir.AluOpType
+
+ROWS = 1024
+FEATURES = 1024
+HIDDEN = 1024
+
+P = 128
+PACK = 4
+K_PASS = P * PACK
+PASSES = ROWS // K_PASS
+M_TILE = 128
+M_TILES = FEATURES // M_TILE
+N_WINDOW = 512
+RUN = 4
+X_PIECE = 512
+
+COLUMN_GROUPS = (512, 512)
+assert sum(COLUMN_GROUPS) == HIDDEN and COLUMN_GROUPS[0] == N_WINDOW
+
+FLOPS = 2 * ROWS * FEATURES * HIDDEN
+BYTES = 4 * ROWS * 1024 * 2 + 2 * ROWS * 1024 * 4
+
+
+def rows_view(rows_tile):
+    return rows_tile.rearrange("p j (r i) -> p r j i", i=RUN)
+
+
+def grouped_view(grouped_tile):
+    return grouped_tile.rearrange("p (r i) j -> p r j i", i=RUN)
+
+
+def tile_grulrcell_pb_v_kernel(
+    tc, x, state, cand, w2, u2, bias_gate, z, grad_out, out
+):
+    nc = tc.nc
+
+    chunks = []
+    first_column = 0
+    for width in COLUMN_GROUPS:
+        for c in range(PASSES):
+            chunks.append((first_column, width, c))
+        first_column += width
+    n_chunks = len(chunks)
+
+    with ExitStack() as ctx:
+        ctx.enter_context(tc.manual_schedule())
+        loads = ctx.enter_context(tc.tile_pool(name="loads", bufs=1))
+        keep = ctx.enter_context(tc.tile_pool(name="keep", bufs=1))
+        work = ctx.enter_context(tc.tile_pool(name="work", bufs=2))
+        results = ctx.enter_context(tc.tile_pool(name="results", bufs=M_TILES))
+        psum = ctx.enter_context(tc.psum_pool(name="psum", bufs=M_TILES))
+
+        def load_rows(name, dram, dtype, c, column, width):
+            rows_tile = loads.tile([P, PACK, width], dtype, name=name)
+            nc.sync.dma_start(
+                out=rows_tile[:],
+                in_=dram[c * K_PASS : (c + 1) * K_PASS, column : column + width].rearrange(
+                    "(p j) w -> p j w", j=PACK
+                ),
+            )
+            return rows_tile
+
+        z_rows, state_rows, cand_rows, grad_rows, x_rows = {}, {}, {}, {}, {}
+        for k in range(n_chunks + 1):
+            if k < n_chunks:
+                column, width, c = chunks[k]
+                z_rows[k] = load_rows("z%d" % k, z, F32, c, column, width)
+                state_rows[k] = load_rows("state%d" % k, state, BF16, c, column, width)
+                cand_rows[k] = load_rows("cand%d" % k, cand, BF16, c, column, width)
+            if k >= 1:
+                column, width, c = chunks[k - 1]
+                grad_rows[k - 1] = load_rows("grad%d" % (k - 1), grad_out, BF16, c, column, width)
+            if 1 <= k <= PASSES:
+                x_rows[k - 1] = load_rows("x%d" % (k - 1), x, BF16, k - 1, 0, FEATURES)
+
+        x_grouped = {}
+        for c in range(PASSES):
+            x_grouped[c] = keep.tile(
+                [P, FEATURES, PACK], BF16, name="x_grouped%d" % c, align_bytes=64
+            )
+            for column in range(0, FEATURES, X_PIECE):
+                nc.scalar.copy(
+                    out=grouped_view(x_grouped[c][:, column : column + X_PIECE, :]),
+                    in_=rows_view(x_rows[c][:, :, column : column + X_PIECE]),
+                )
+
+        x_codes = keep.tile([P, PASSES, FEATURES], U32, align_bytes=64)
+        x_scales = keep.tile([P, PASSES, FEATURES], U8, align_bytes=64)
+        da_codes = keep.tile([P, PASSES, HIDDEN], U32, align_bytes=64)
+        da_scales = keep.tile([P, PASSES, HIDDEN], U8, align_bytes=64)
+
+        def quantise_x(c):
+            nc.vector.quantize_mx(
+                out=x_codes[:, c, :].bitcast(E4M3_X4),
+                scales=x_scales[:, c, :],
+                in_=x_grouped[c][:].rearrange("p w j -> p (w j)"),
+            )
+
+        slope, difference, product, da = {}, {}, {}, {}
+
+        def gate_slope(k):
+            width = chunks[k][1]
+            slope[k] = work.tile([P, PACK, width], F32, name="slope%d" % k, tag="slope")
+            nc.vector.scalar_tensor_tensor(
+                out=slope[k][:],
+                in0=z_rows[k][:],
+                scalar=1.0,
+                in1=z_rows[k][:],
+                op0=ALU.subtract,
+                op1=ALU.mult,
+            )
+
+        def state_difference(k):
+            width = chunks[k][1]
+            difference[k] = work.tile(
+                [P, PACK, width], F32, name="difference%d" % k, tag="difference"
+            )
+            nc.vector.tensor_tensor(
+                out=difference[k][:], in0=cand_rows[k][:], in1=state_rows[k][:], op=ALU.subtract
+            )
+
+        def slope_times_difference(k):
+            width = chunks[k][1]
+            product[k] = work.tile([P, PACK, width], F32, name="product%d" % k, tag="product")
+            nc.vector.tensor_tensor(
+                out=product[k][:], in0=slope[k][:], in1=difference[k][:], op=ALU.mult
+            )
+
+        def times_grad_out(k):
+            width = chunks[k][1]
+            da[k] = work.tile([P, width, PACK], BF16, name="da%d" % k, tag="da", align_bytes=64)
+            nc.vector.tensor_tensor(
+                out=grouped_view(da[k][:]),
+                in0=rows_view(product[k][:]),
+                in1=rows_view(grad_rows[k][:]),
+                op=ALU.mult,
+            )
+
+        def quantise_da(k):
+            column, width, c = chunks[k]
+            nc.vector.quantize_mx(
+                out=da_codes[:, c, column : column + width].bitcast(E5M2_X4),
+                scales=da_scales[:, c, column : column + width],
+                in_=da[k][:].rearrange("p w j -> p (w j)"),
+            )
+
+        sums = {}
+
+        def multiply(k):
+            column, width, c = chunks[k]
+            window = slice(column + width - N_WINDOW, column + width)
+            for m in range(M_TILES):
+                if c == 0:
+                    sums[m] = psum.tile([M_TILE, N_WINDOW], F32, name="sums%d_%d" % (k, m), tag="sums")
+                features = slice(m * M_TILE, (m + 1) * M_TILE)
+                nc.tensor.matmul_mx(
+                    out=sums[m][:],
+                    lhsT=x_codes[:, c, features].bitcast(E4M3_X4),
+                    lhsT_scale=x_scales[:, c, features],
+                    rhs=da_codes[:, c, window].bitcast(E5M2_X4),
+                    rhs_scale=da_scales[:, c, window],
+                    start=(c == 0),
+                    stop=(c == PASSES - 1),
+                )
+
+        def store_group(k):
+            column, width, c = chunks[k]
+            for m in range(M_TILES):
+                result = results.tile([M_TILE, width], F32, name="result%d_%d" % (k, m), tag="result")
+                if k == n_chunks - 1 and m % 2 == 1:
+                    nc.vector.tensor_copy(out=result[:], in_=sums[m][:, N_WINDOW - width :])
+                else:
+                    nc.scalar.copy(out=result[:], in_=sums[m][:, N_WINDOW - width :])
+                nc.sync.dma_start(
+                    out=out[m * M_TILE : (m + 1) * M_TILE, column : column + width], in_=result[:]
+                )
+
+        for k in range(n_chunks + 1):
+            if k < n_chunks:
+                gate_slope(k)
+                state_difference(k)
+            if k >= 1:
+                times_grad_out(k - 1)
+            if k < n_chunks:
+                slope_times_difference(k)
+            if k >= 1:
+                quantise_da(k - 1)
+            if k == PASSES:
+                for c in range(PASSES):
+                    quantise_x(c)
+                for c in range(PASSES):
+                    multiply(c)
+                store_group(PASSES - 1)
+            if k > PASSES:
+                multiply(k - 1)
+                if chunks[k - 1][2] == PASSES - 1:
+                    store_group(k - 1)

@@ -23,8 +23,9 @@ M_TILES = FEATURES // M_TILE
 N_WINDOW = 512
 RUN = 4
 X_PIECE = 512
+LOAD_WIDTH = 512
 
-COLUMN_GROUPS = (512, 512)
+COLUMN_GROUPS = (512, 256, 256)
 assert sum(COLUMN_GROUPS) == HIDDEN and COLUMN_GROUPS[0] == N_WINDOW
 
 FLOPS = 2 * ROWS * FEATURES * HIDDEN
@@ -70,18 +71,24 @@ def tile_grulrcell_pb_v_kernel(
             )
             return rows_tile
 
+        load_keys = [(column, c) for column in range(0, HIDDEN, LOAD_WIDTH) for c in range(PASSES)]
         z_rows, state_rows, cand_rows, grad_rows, x_rows = {}, {}, {}, {}, {}
-        for k in range(n_chunks + 1):
-            if k < n_chunks:
-                column, width, c = chunks[k]
-                z_rows[k] = load_rows("z%d" % k, z, F32, c, column, width)
-                state_rows[k] = load_rows("state%d" % k, state, BF16, c, column, width)
-                cand_rows[k] = load_rows("cand%d" % k, cand, BF16, c, column, width)
-            if k >= 1:
-                column, width, c = chunks[k - 1]
-                grad_rows[k - 1] = load_rows("grad%d" % (k - 1), grad_out, BF16, c, column, width)
-            if 1 <= k <= PASSES:
-                x_rows[k - 1] = load_rows("x%d" % (k - 1), x, BF16, k - 1, 0, FEATURES)
+        for n in range(len(load_keys) + 1):
+            if n < len(load_keys):
+                column, c = load_keys[n]
+                z_rows[column, c] = load_rows("z%d" % n, z, F32, c, column, LOAD_WIDTH)
+                state_rows[column, c] = load_rows("state%d" % n, state, BF16, c, column, LOAD_WIDTH)
+                cand_rows[column, c] = load_rows("cand%d" % n, cand, BF16, c, column, LOAD_WIDTH)
+            if n >= 1:
+                column, c = load_keys[n - 1]
+                grad_rows[column, c] = load_rows("grad%d" % (n - 1), grad_out, BF16, c, column, LOAD_WIDTH)
+            if 1 <= n <= PASSES:
+                x_rows[n - 1] = load_rows("x%d" % (n - 1), x, BF16, n - 1, 0, FEATURES)
+
+        def of_chunk(loaded, k):
+            column, width, c = chunks[k]
+            offset = column % LOAD_WIDTH
+            return loaded[column - offset, c][:, :, offset : offset + width]
 
         x_grouped = {}
         for c in range(PASSES):
@@ -113,9 +120,9 @@ def tile_grulrcell_pb_v_kernel(
             slope[k] = work.tile([P, PACK, width], F32, name="slope%d" % k, tag="slope")
             nc.vector.scalar_tensor_tensor(
                 out=slope[k][:],
-                in0=z_rows[k][:],
+                in0=of_chunk(z_rows, k),
                 scalar=1.0,
-                in1=z_rows[k][:],
+                in1=of_chunk(z_rows, k),
                 op0=ALU.subtract,
                 op1=ALU.mult,
             )
@@ -126,7 +133,10 @@ def tile_grulrcell_pb_v_kernel(
                 [P, PACK, width], F32, name="difference%d" % k, tag="difference"
             )
             nc.vector.tensor_tensor(
-                out=difference[k][:], in0=cand_rows[k][:], in1=state_rows[k][:], op=ALU.subtract
+                out=difference[k][:],
+                in0=of_chunk(cand_rows, k),
+                in1=of_chunk(state_rows, k),
+                op=ALU.subtract,
             )
 
         def slope_times_difference(k):
@@ -142,7 +152,7 @@ def tile_grulrcell_pb_v_kernel(
             nc.vector.tensor_tensor(
                 out=grouped_view(da[k][:]),
                 in0=rows_view(product[k][:]),
-                in1=rows_view(grad_rows[k][:]),
+                in1=rows_view(of_chunk(grad_rows, k)),
                 op=ALU.mult,
             )
 

@@ -25,8 +25,10 @@ RUN = 4
 X_PIECE = 512
 LOAD_WIDTH = 512
 
-COLUMN_GROUPS = (512, 256, 256)
-assert sum(COLUMN_GROUPS) == HIDDEN and COLUMN_GROUPS[0] == N_WINDOW
+GROUPS_OF_LOAD = ((512,), (256, 256))
+assert len(GROUPS_OF_LOAD) * LOAD_WIDTH == HIDDEN
+assert all(sum(widths) == LOAD_WIDTH for widths in GROUPS_OF_LOAD)
+assert GROUPS_OF_LOAD[0][0] == N_WINDOW
 
 FLOPS = 2 * ROWS * FEATURES * HIDDEN
 BYTES = 4 * ROWS * 1024 * 2 + 2 * ROWS * 1024 * 4
@@ -45,13 +47,32 @@ def tile_grulrcell_pb_v_kernel(
 ):
     nc = tc.nc
 
+    load_keys = []
+    groups = []
     chunks = []
-    first_column = 0
-    for width in COLUMN_GROUPS:
+    for n, widths in enumerate(GROUPS_OF_LOAD):
+        groups_here = []
+        column = n * LOAD_WIDTH
+        for width in widths:
+            groups_here.append((column, width))
+            column += width
+        groups.extend(groups_here)
         for c in range(PASSES):
-            chunks.append((first_column, width, c))
-        first_column += width
+            load_keys.append((n * LOAD_WIDTH, c))
+        for column, width in groups_here:
+            for c in range(PASSES):
+                chunks.append((column, width, c))
     n_chunks = len(chunks)
+    chunks_of_first_load = PASSES * len(GROUPS_OF_LOAD[0])
+
+    def row_cuts(key):
+        if key == load_keys[0]:
+            return [slice(j, j + 1) for j in range(PACK)]
+        return [slice(0, PACK)]
+
+    def key_of_chunk(k):
+        column, width, c = chunks[k]
+        return (column - column % LOAD_WIDTH, c)
 
     with ExitStack() as ctx:
         ctx.enter_context(tc.manual_schedule())
@@ -61,34 +82,37 @@ def tile_grulrcell_pb_v_kernel(
         results = ctx.enter_context(tc.tile_pool(name="results", bufs=M_TILES))
         psum = ctx.enter_context(tc.psum_pool(name="psum", bufs=M_TILES))
 
-        def load_rows(name, dram, dtype, c, column, width):
-            rows_tile = loads.tile([P, PACK, width], dtype, name=name)
-            nc.sync.dma_start(
-                out=rows_tile[:],
-                in_=dram[c * K_PASS : (c + 1) * K_PASS, column : column + width].rearrange(
-                    "(p j) w -> p j w", j=PACK
-                ),
+        def load(rows_tile, dram, key, width, rows):
+            column, c = key
+            source = dram[c * K_PASS : (c + 1) * K_PASS, column : column + width].rearrange(
+                "(p j) w -> p j w", j=PACK
             )
-            return rows_tile
+            nc.sync.dma_start(out=rows_tile[:, rows, :], in_=source[:, rows, :])
 
-        load_keys = [(column, c) for column in range(0, HIDDEN, LOAD_WIDTH) for c in range(PASSES)]
         z_rows, state_rows, cand_rows, grad_rows, x_rows = {}, {}, {}, {}, {}
         for n in range(len(load_keys) + 1):
             if n < len(load_keys):
-                column, c = load_keys[n]
-                z_rows[column, c] = load_rows("z%d" % n, z, F32, c, column, LOAD_WIDTH)
-                state_rows[column, c] = load_rows("state%d" % n, state, BF16, c, column, LOAD_WIDTH)
-                cand_rows[column, c] = load_rows("cand%d" % n, cand, BF16, c, column, LOAD_WIDTH)
+                key = load_keys[n]
+                z_rows[key] = loads.tile([P, PACK, LOAD_WIDTH], F32, name="z%d" % n)
+                state_rows[key] = loads.tile([P, PACK, LOAD_WIDTH], BF16, name="state%d" % n)
+                cand_rows[key] = loads.tile([P, PACK, LOAD_WIDTH], BF16, name="cand%d" % n)
+                grad_rows[key] = loads.tile([P, PACK, LOAD_WIDTH], BF16, name="grad%d" % n)
+                for rows in row_cuts(key):
+                    load(z_rows[key], z, key, LOAD_WIDTH, rows)
             if n >= 1:
-                column, c = load_keys[n - 1]
-                grad_rows[column, c] = load_rows("grad%d" % (n - 1), grad_out, BF16, c, column, LOAD_WIDTH)
+                load(grad_rows[load_keys[n - 1]], grad_out, load_keys[n - 1], LOAD_WIDTH, slice(0, PACK))
+            if n < len(load_keys):
+                for rows in row_cuts(key):
+                    load(state_rows[key], state, key, LOAD_WIDTH, rows)
+                    load(cand_rows[key], cand, key, LOAD_WIDTH, rows)
             if 1 <= n <= PASSES:
-                x_rows[n - 1] = load_rows("x%d" % (n - 1), x, BF16, n - 1, 0, FEATURES)
+                x_rows[n - 1] = loads.tile([P, PACK, FEATURES], BF16, name="x%d" % (n - 1))
+                load(x_rows[n - 1], x, (0, n - 1), FEATURES, slice(0, PACK))
 
         def of_chunk(loaded, k):
             column, width, c = chunks[k]
             offset = column % LOAD_WIDTH
-            return loaded[column - offset, c][:, :, offset : offset + width]
+            return loaded[key_of_chunk(k)][:, :, offset : offset + width]
 
         x_grouped = {}
         for c in range(PASSES):
@@ -118,26 +142,28 @@ def tile_grulrcell_pb_v_kernel(
         def gate_slope(k):
             width = chunks[k][1]
             slope[k] = work.tile([P, PACK, width], F32, name="slope%d" % k, tag="slope")
-            nc.vector.scalar_tensor_tensor(
-                out=slope[k][:],
-                in0=of_chunk(z_rows, k),
-                scalar=1.0,
-                in1=of_chunk(z_rows, k),
-                op0=ALU.subtract,
-                op1=ALU.mult,
-            )
+            for rows in row_cuts(key_of_chunk(k)):
+                nc.vector.scalar_tensor_tensor(
+                    out=slope[k][:, rows, :],
+                    in0=of_chunk(z_rows, k)[:, rows, :],
+                    scalar=1.0,
+                    in1=of_chunk(z_rows, k)[:, rows, :],
+                    op0=ALU.subtract,
+                    op1=ALU.mult,
+                )
 
         def state_difference(k):
             width = chunks[k][1]
             difference[k] = work.tile(
                 [P, PACK, width], F32, name="difference%d" % k, tag="difference"
             )
-            nc.vector.tensor_tensor(
-                out=difference[k][:],
-                in0=of_chunk(cand_rows, k),
-                in1=of_chunk(state_rows, k),
-                op=ALU.subtract,
-            )
+            for rows in row_cuts(key_of_chunk(k)):
+                nc.vector.tensor_tensor(
+                    out=difference[k][:, rows, :],
+                    in0=of_chunk(cand_rows, k)[:, rows, :],
+                    in1=of_chunk(state_rows, k)[:, rows, :],
+                    op=ALU.subtract,
+                )
 
         def slope_times_difference(k):
             width = chunks[k][1]
@@ -164,54 +190,47 @@ def tile_grulrcell_pb_v_kernel(
                 in_=da[k][:].rearrange("p w j -> p (w j)"),
             )
 
-        sums = {}
+        for k in range(n_chunks + 1):
+            if k < n_chunks:
+                gate_slope(k)
+            if k >= 1:
+                times_grad_out(k - 1)
+            if k < n_chunks:
+                state_difference(k)
+            if k >= 1:
+                quantise_da(k - 1)
+            if 0 <= k - chunks_of_first_load < PASSES:
+                quantise_x(k - chunks_of_first_load)
+            if k < n_chunks:
+                slope_times_difference(k)
 
-        def multiply(k):
-            column, width, c = chunks[k]
+        for column, width in groups:
             window = slice(column + width - N_WINDOW, column + width)
+            sums = {}
+            for c in range(PASSES):
+                for m in range(M_TILES):
+                    if c == 0:
+                        sums[m] = psum.tile(
+                            [M_TILE, N_WINDOW], F32, name="sums%d_%d" % (column, m), tag="sums"
+                        )
+                    features = slice(m * M_TILE, (m + 1) * M_TILE)
+                    nc.tensor.matmul_mx(
+                        out=sums[m][:],
+                        lhsT=x_codes[:, c, features].bitcast(E4M3_X4),
+                        lhsT_scale=x_scales[:, c, features],
+                        rhs=da_codes[:, c, window].bitcast(E5M2_X4),
+                        rhs_scale=da_scales[:, c, window],
+                        start=(c == 0),
+                        stop=(c == PASSES - 1),
+                    )
             for m in range(M_TILES):
-                if c == 0:
-                    sums[m] = psum.tile([M_TILE, N_WINDOW], F32, name="sums%d_%d" % (k, m), tag="sums")
-                features = slice(m * M_TILE, (m + 1) * M_TILE)
-                nc.tensor.matmul_mx(
-                    out=sums[m][:],
-                    lhsT=x_codes[:, c, features].bitcast(E4M3_X4),
-                    lhsT_scale=x_scales[:, c, features],
-                    rhs=da_codes[:, c, window].bitcast(E5M2_X4),
-                    rhs_scale=da_scales[:, c, window],
-                    start=(c == 0),
-                    stop=(c == PASSES - 1),
+                result = results.tile(
+                    [M_TILE, width], F32, name="result%d_%d" % (column, m), tag="result"
                 )
-
-        def store_group(k):
-            column, width, c = chunks[k]
-            for m in range(M_TILES):
-                result = results.tile([M_TILE, width], F32, name="result%d_%d" % (k, m), tag="result")
-                if k == n_chunks - 1 and m % 2 == 1:
+                if column + width == HIDDEN and m % 2 == 1:
                     nc.vector.tensor_copy(out=result[:], in_=sums[m][:, N_WINDOW - width :])
                 else:
                     nc.scalar.copy(out=result[:], in_=sums[m][:, N_WINDOW - width :])
                 nc.sync.dma_start(
                     out=out[m * M_TILE : (m + 1) * M_TILE, column : column + width], in_=result[:]
                 )
-
-        for k in range(n_chunks + 1):
-            if k < n_chunks:
-                gate_slope(k)
-                state_difference(k)
-            if k >= 1:
-                times_grad_out(k - 1)
-            if k < n_chunks:
-                slope_times_difference(k)
-            if k >= 1:
-                quantise_da(k - 1)
-            if k == PASSES:
-                for c in range(PASSES):
-                    quantise_x(c)
-                for c in range(PASSES):
-                    multiply(c)
-                store_group(PASSES - 1)
-            if k > PASSES:
-                multiply(k - 1)
-                if chunks[k - 1][2] == PASSES - 1:
-                    store_group(k - 1)

from contextlib import ExitStack

import concourse.mybir as mybir

F32 = mybir.dt.float32
BF16 = mybir.dt.bfloat16
U32 = mybir.dt.uint32
U8 = mybir.dt.uint8
E4M3_X4 = mybir.dt.float8_e4m3fn_x4
E5M2_X4 = mybir.dt.float8_e5m2_x4
ALU = mybir.AluOpType

ROWS = 1024
FEATURES = 1024
HIDDEN = 1024

P = 128
PACK = 4
K_PASS = P * PACK
PASSES = ROWS // K_PASS
M_TILE = 128
M_TILES = FEATURES // M_TILE
N_WINDOW = 512
RUN = 4
X_PIECE = 512
LOAD_WIDTH = 512

GROUPS_OF_LOAD = ((512,), (256, 256))
assert len(GROUPS_OF_LOAD) * LOAD_WIDTH == HIDDEN
assert all(sum(widths) == LOAD_WIDTH for widths in GROUPS_OF_LOAD)
assert GROUPS_OF_LOAD[0][0] == N_WINDOW

FLOPS = 2 * ROWS * FEATURES * HIDDEN
BYTES = 4 * ROWS * 1024 * 2 + 2 * ROWS * 1024 * 4


def rows_view(rows_tile):
    return rows_tile.rearrange("p j (r i) -> p r j i", i=RUN)


def grouped_view(grouped_tile):
    return grouped_tile.rearrange("p (r i) j -> p r j i", i=RUN)


def tile_grulrcell_pb_v_kernel(
    tc, x, state, cand, w2, u2, bias_gate, z, grad_out, out
):
    nc = tc.nc

    load_keys = []
    groups = []
    chunks = []
    for n, widths in enumerate(GROUPS_OF_LOAD):
        groups_here = []
        column = n * LOAD_WIDTH
        for width in widths:
            groups_here.append((column, width))
            column += width
        groups.extend(groups_here)
        for c in range(PASSES):
            load_keys.append((n * LOAD_WIDTH, c))
        for column, width in groups_here:
            for c in range(PASSES):
                chunks.append((column, width, c))
    n_chunks = len(chunks)
    chunks_of_first_load = PASSES * len(GROUPS_OF_LOAD[0])

    def row_cuts(key):
        if key == load_keys[0]:
            return [slice(j, j + 1) for j in range(PACK)]
        return [slice(0, PACK)]

    def key_of_chunk(k):
        column, width, c = chunks[k]
        return (column - column % LOAD_WIDTH, c)

    with ExitStack() as ctx:
        ctx.enter_context(tc.manual_schedule())
        loads = ctx.enter_context(tc.tile_pool(name="loads", bufs=1))
        keep = ctx.enter_context(tc.tile_pool(name="keep", bufs=1))
        work = ctx.enter_context(tc.tile_pool(name="work", bufs=2))
        results = ctx.enter_context(tc.tile_pool(name="results", bufs=M_TILES))
        psum = ctx.enter_context(tc.psum_pool(name="psum", bufs=M_TILES))

        def load(rows_tile, dram, key, width, rows):
            column, c = key
            source = dram[c * K_PASS : (c + 1) * K_PASS, column : column + width].rearrange(
                "(p j) w -> p j w", j=PACK
            )
            nc.sync.dma_start(out=rows_tile[:, rows, :], in_=source[:, rows, :])

        z_rows, state_rows, cand_rows, grad_rows, x_rows = {}, {}, {}, {}, {}
        for n in range(len(load_keys) + 1):
            if n < len(load_keys):
                key = load_keys[n]
                z_rows[key] = loads.tile([P, PACK, LOAD_WIDTH], F32, name="z%d" % n)
                state_rows[key] = loads.tile([P, PACK, LOAD_WIDTH], BF16, name="state%d" % n)
                cand_rows[key] = loads.tile([P, PACK, LOAD_WIDTH], BF16, name="cand%d" % n)
                grad_rows[key] = loads.tile([P, PACK, LOAD_WIDTH], BF16, name="grad%d" % n)
                for rows in row_cuts(key):
                    load(z_rows[key], z, key, LOAD_WIDTH, rows)
            if n >= 1:
                load(grad_rows[load_keys[n - 1]], grad_out, load_keys[n - 1], LOAD_WIDTH, slice(0, PACK))
            if n < len(load_keys):
                for rows in row_cuts(key):
                    load(state_rows[key], state, key, LOAD_WIDTH, rows)
                    load(cand_rows[key], cand, key, LOAD_WIDTH, rows)
            if 1 <= n <= PASSES:
                x_rows[n - 1] = loads.tile([P, PACK, FEATURES], BF16, name="x%d" % (n - 1))
                load(x_rows[n - 1], x, (0, n - 1), FEATURES, slice(0, PACK))

        def of_chunk(loaded, k):
            column, width, c = chunks[k]
            offset = column % LOAD_WIDTH
            return loaded[key_of_chunk(k)][:, :, offset : offset + width]

        x_grouped = {}
        for c in range(PASSES):
            x_grouped[c] = keep.tile(
                [P, FEATURES, PACK], BF16, name="x_grouped%d" % c, align_bytes=64
            )
            for column in range(0, FEATURES, X_PIECE):
                nc.scalar.copy(
                    out=grouped_view(x_grouped[c][:, column : column + X_PIECE, :]),
                    in_=rows_view(x_rows[c][:, :, column : column + X_PIECE]),
                )

        x_codes = keep.tile([P, PASSES, FEATURES], U32, align_bytes=64)
        x_scales = keep.tile([P, PASSES, FEATURES], U8, align_bytes=64)
        da_codes = keep.tile([P, PASSES, HIDDEN], U32, align_bytes=64)
        da_scales = keep.tile([P, PASSES, HIDDEN], U8, align_bytes=64)

        def quantise_x(c):
            nc.vector.quantize_mx(
                out=x_codes[:, c, :].bitcast(E4M3_X4),
                scales=x_scales[:, c, :],
                in_=x_grouped[c][:].rearrange("p w j -> p (w j)"),
            )

        slope, difference, product, da = {}, {}, {}, {}

        def gate_slope(k):
            width = chunks[k][1]
            slope[k] = work.tile([P, PACK, width], F32, name="slope%d" % k, tag="slope")
            for rows in row_cuts(key_of_chunk(k)):
                nc.vector.scalar_tensor_tensor(
                    out=slope[k][:, rows, :],
                    in0=of_chunk(z_rows, k)[:, rows, :],
                    scalar=1.0,
                    in1=of_chunk(z_rows, k)[:, rows, :],
                    op0=ALU.subtract,
                    op1=ALU.mult,
                )

        def state_difference(k):
            width = chunks[k][1]
            difference[k] = work.tile(
                [P, PACK, width], F32, name="difference%d" % k, tag="difference"
            )
            for rows in row_cuts(key_of_chunk(k)):
                nc.vector.tensor_tensor(
                    out=difference[k][:, rows, :],
                    in0=of_chunk(cand_rows, k)[:, rows, :],
                    in1=of_chunk(state_rows, k)[:, rows, :],
                    op=ALU.subtract,
                )

        def slope_times_difference(k):
            width = chunks[k][1]
            product[k] = work.tile([P, PACK, width], F32, name="product%d" % k, tag="product")
            nc.vector.tensor_tensor(
                out=product[k][:], in0=slope[k][:], in1=difference[k][:], op=ALU.mult
            )

        def times_grad_out(k):
            width = chunks[k][1]
            da[k] = work.tile([P, width, PACK], BF16, name="da%d" % k, tag="da", align_bytes=64)
            nc.vector.tensor_tensor(
                out=grouped_view(da[k][:]),
                in0=rows_view(product[k][:]),
                in1=rows_view(of_chunk(grad_rows, k)),
                op=ALU.mult,
            )

        def quantise_da(k):
            column, width, c = chunks[k]
            nc.vector.quantize_mx(
                out=da_codes[:, c, column : column + width].bitcast(E5M2_X4),
                scales=da_scales[:, c, column : column + width],
                in_=da[k][:].rearrange("p w j -> p (w j)"),
            )

        for k in range(n_chunks + 1):
            if k < n_chunks:
                gate_slope(k)
            if k >= 1:
                times_grad_out(k - 1)
            if k < n_chunks:
                state_difference(k)
            if k >= 1:
                quantise_da(k - 1)
            if 0 <= k - chunks_of_first_load < PASSES:
                quantise_x(k - chunks_of_first_load)
            if k < n_chunks:
                slope_times_difference(k)

        for column, width in groups:
            window = slice(column + width - N_WINDOW, column + width)
            sums = {}
            for c in range(PASSES):
                for m in range(M_TILES):
                    if c == 0:
                        sums[m] = psum.tile(
                            [M_TILE, N_WINDOW], F32, name="sums%d_%d" % (column, m), tag="sums"
                        )
                    features = slice(m * M_TILE, (m + 1) * M_TILE)
                    nc.tensor.matmul_mx(
                        out=sums[m][:],
                        lhsT=x_codes[:, c, features].bitcast(E4M3_X4),
                        lhsT_scale=x_scales[:, c, features],
                        rhs=da_codes[:, c, window].bitcast(E5M2_X4),
                        rhs_scale=da_scales[:, c, window],
                        start=(c == 0),
                        stop=(c == PASSES - 1),
                    )
            for m in range(M_TILES):
                result = results.tile(
                    [M_TILE, width], F32, name="result%d_%d" % (column, m), tag="result"
                )
                if column + width == HIDDEN and m % 2 == 1:
                    nc.vector.tensor_copy(out=result[:], in_=sums[m][:, N_WINDOW - width :])
                else:
                    nc.scalar.copy(out=result[:], in_=sums[m][:, N_WINDOW - width :])
                nc.sync.dma_start(
                    out=out[m * M_TILE : (m + 1) * M_TILE, column : column + width], in_=result[:]
                )
